import numpy as np
import ml_dtypes


def mxq(x, axis, fmt="e4m3"):
    dtype, down = {"e4m3": (ml_dtypes.float8_e4m3fn, 7), "e5m2": (ml_dtypes.float8_e5m2, 14)}[fmt]
    v = np.moveaxis(np.asarray(x, np.float32).astype(ml_dtypes.bfloat16).astype(np.float64), axis, -1)
    blocks = v.reshape(v.shape[:-1] + (-1, 32))
    amax = np.abs(blocks).max(-1, keepdims=True)
    byte = np.maximum(np.where(amax > 0, np.frexp(amax)[1] - 1 + 127, 0) - down, 1)
    scale = np.exp2(byte - 127.0)
    codes = (blocks / scale).astype(np.float32).astype(dtype).astype(np.float64)
    return np.moveaxis((codes * scale).reshape(v.shape), -1, axis)


WIDE = False


def mx_kscale(k):
    if not WIDE:
        return np.ones(k)
    levels = np.array([10, -10, 5, -5, 0])
    a = np.random.permutation(np.resize(levels, k // 512 * 4)).reshape(k // 512, 4)
    idx = np.arange(k)
    return np.exp2(a[idx // 512, idx % 128 // 32])


BF16 = ml_dtypes.bfloat16


def bf(x):
    return np.asarray(x, np.float32).astype(BF16)


def f64(x):
    return np.asarray(x).astype(np.float64)


E2M1 = np.array([0.0, 0.5, 1.0, 1.5, 2.0, 3.0, 4.0, 6.0, -0.0, -0.5, -1.0, -1.5, -2.0, -3.0, -4.0, -6.0])


def pack_weight(w, fmt):
    k, n = w.shape
    w = f64(bf(w)).reshape(k // 32, 32, n)
    amax = np.abs(w).max(1)
    if fmt == "e4m3":
        byte = np.frexp(amax)[1] - 1 + 127 - 7
    else:
        mant, ex = np.frexp(amax / 6.0)
        byte = np.where(mant > 0.5, ex, ex - 1) + 127
    byte = np.clip(np.where(amax > 0, byte, 1), 1, 254)
    scaled = (w * np.exp2(127.0 - byte)[:, None, :]).reshape(k, n).astype(np.float32)
    by_word = np.ascontiguousarray(scaled.reshape(k // 512, 128, 4, n).transpose(0, 1, 3, 2))
    if fmt == "e4m3":
        words = by_word.astype(ml_dtypes.float8_e4m3fn).view(np.uint8)
    else:
        c = by_word.astype(ml_dtypes.float4_e2m1fn).view(np.uint8) & 0xF
        words = c[..., 0::2] | (c[..., 1::2] << 4)
    return np.ascontiguousarray(words), np.ascontiguousarray(byte.astype(np.uint8).reshape(k // 512, 16, n))


def unpack_weight(words, scales, fmt):
    g, p, n, _ = words.shape
    if fmt == "e4m3":
        vals = np.ascontiguousarray(words).view(ml_dtypes.float8_e4m3fn).astype(np.float64)
    else:
        nib = np.empty((g, p, n, 4), np.uint8)
        nib[..., 0::2] = words & 0xF
        nib[..., 1::2] = words >> 4
        vals = E2M1[nib]
    vals = vals * np.repeat(np.exp2(scales.astype(np.float64) - 127.0), 8, axis=1)[..., None]
    return vals.transpose(0, 1, 3, 2).reshape(g * 512, n)

def pack4(w):
    words, scales = pack_weight(w, "e2m1")
    return words.reshape(words.shape[0], 128, -1), scales


def unpack4(words, scales):
    return unpack_weight(words.reshape(words.shape[0], 128, -1, 2), scales, "e2m1")


B, C, H, W = 2, 512, 64, 64


def setup_inputs():
    t = np.exp2(np.round(np.log2(mx_kscale(C)) / 2))
    x = np.random.standard_normal((B, C, H, W)) * t[None, :, None, None]
    beta = 1.0 + 0.1 * np.random.standard_normal((1, C, 1, 1))
    gamma = (0.25 * np.eye(C) + np.exp(2.0 * np.random.standard_normal((C, C)) - 2.0) / C) / (t * t)[None, :]
    gamma_words, gamma_scales = pack4(np.ascontiguousarray(gamma.T))
    return {"x": bf(x), "beta": bf(beta), "gamma_words": gamma_words, "gamma_scales": gamma_scales}


def reference(x, beta, gamma_words, gamma_scales):
    x = f64(x)
    g = unpack4(gamma_words, gamma_scales).T
    xx = (x * x).reshape(B, C, H * W)
    mix = (g @ mxq(xx, 1, "e4m3")).reshape(B, C, H, W)
    norm = np.sqrt(f64(beta) + mix)
    return x / norm

@@ -1,0 +1,103 @@
+from contextlib import ExitStack
+
+import concourse.mybir as mybir
+
+F32 = mybir.dt.float32
+BF16 = mybir.dt.bfloat16
+I32 = mybir.dt.int32
+U32 = mybir.dt.uint32
+U8 = mybir.dt.uint8
+FP8X4 = mybir.dt.float8_e4m3fn_x4
+FP4X4 = mybir.dt.float4_e2m1fn_x4
+ACT = mybir.ActivationFunctionType
+ALU = mybir.AluOpType
+
+P = 128
+PACK = 4
+BATCH = 2
+CHANNELS = 512
+POSITIONS = 64 * 64
+OUT_TILES = CHANNELS // P
+N_PASS = 512
+CHUNK = 1024
+SCALAR_COLS = 640
+
+FLOPS = 2 * CHANNELS * CHANNELS * BATCH * POSITIONS
+
+
+def tile_gdn_kernel(tc, x, beta, gamma_words, gamma_scales, out):
+    nc = tc.nc
+    x_by_word = x.rearrange("b (p t) h w -> b p t (h w)", t=PACK)
+    x_by_tile = x.rearrange("b (j m) h w -> b m j (h w)", m=P)
+    out_by_tile = out.rearrange("b (j m) h w -> b m j (h w)", m=P)
+
+    with ExitStack() as ctx:
+        const = ctx.enter_context(tc.tile_pool(name="const", bufs=1))
+        loads = ctx.enter_context(tc.tile_pool(name="loads", bufs=4))
+        quant = ctx.enter_context(tc.tile_pool(name="quant", bufs=2))
+        norms = ctx.enter_context(tc.tile_pool(name="norms", bufs=4))
+        stores = ctx.enter_context(tc.tile_pool(name="stores", bufs=3))
+        psum = ctx.enter_context(tc.psum_pool(name="psum", bufs=8))
+
+        g_words = const.tile([P, 2 * CHANNELS], U8, align_bytes=64)
+        g_scales = const.tile([P, CHANNELS], U8, align_bytes=64)
+        nc.vector.memset(g_scales[:].bitcast(I32), 0)
+        nc.sync.dma_start(out=g_words[:].bitcast(I32), in_=gamma_words[0].bitcast(I32))
+        for quadrant in range(4):
+            nc.sync.dma_start(
+                out=g_scales[32 * quadrant : 32 * quadrant + 4, :].bitcast(I32),
+                in_=gamma_scales[0, 4 * quadrant : 4 * quadrant + 4, :].bitcast(I32),
+            )
+
+        beta_bf16 = const.tile([P, OUT_TILES], BF16)
+        with nc.allow_non_contiguous_dma(reason="512 single elements, once"):
+            nc.scalar.dma_start(out=beta_bf16[:], in_=beta.rearrange("a (j m) h w -> m (a j h w)", m=P))
+        beta_f32 = const.tile([P, OUT_TILES], F32)
+        nc.vector.tensor_copy(out=beta_f32[:], in_=beta_bf16[:])
+
+        for b in range(BATCH):
+            for first in range(0, POSITIONS, CHUNK):
+                cols = slice(first, first + CHUNK)
+                x_word = loads.tile([P, PACK, CHUNK], BF16)
+                nc.sync.dma_start(out=x_word[:], in_=x_by_word[b, :, :, cols])
+                x_tile = loads.tile([P, OUT_TILES, CHUNK], BF16)
+                nc.sync.dma_start(out=x_tile[:], in_=x_by_tile[b, :, :, cols])
+
+                squares = quant.tile([P, CHUNK, PACK], BF16, align_bytes=64)
+                src = x_word[:].rearrange("p t (c i) -> p c t i", i=4)
+                dst = squares[:].rearrange("p (c i) t -> p c t i", i=4)
+                cut = SCALAR_COLS // 4
+                nc.scalar.activation(out=dst[:, :cut], in_=src[:, :cut], func=ACT.Square)
+                nc.vector.tensor_tensor(out=dst[:, cut:], in0=src[:, cut:], in1=src[:, cut:], op=ALU.mult)
+
+                codes = quant.tile([P, CHUNK], U32, align_bytes=64)
+                scales = quant.tile([P, CHUNK], U8, align_bytes=64)
+                nc.vector.quantize_mx(
+                    out=codes[:].bitcast(FP8X4),
+                    scales=scales[:],
+                    in_=squares[:].rearrange("p c t -> p (c t)"),
+                )
+
+                result = stores.tile([P, OUT_TILES, CHUNK], F32)
+                for j in range(OUT_TILES):
+                    rnorm = norms.tile([P, CHUNK], F32)
+                    for n0 in range(0, CHUNK, N_PASS):
+                        mix = psum.tile([P, N_PASS], F32)
+                        nc.tensor.matmul_mx(
+                            out=mix[:],
+                            lhsT=g_words[:, 2 * P * j : 2 * P * (j + 1)].bitcast(FP4X4),
+                            lhsT_scale=g_scales[:, P * j : P * (j + 1)],
+                            rhs=codes[:, n0 : n0 + N_PASS].bitcast(FP8X4),
+                            rhs_scale=scales[:, n0 : n0 + N_PASS],
+                            start=True,
+                            stop=True,
+                        )
+                        nc.scalar.activation(
+                            out=rnorm[:, n0 : n0 + N_PASS],
+                            in_=mix[:],
+                            func=ACT.Abs_reciprocal_sqrt,
+                            bias=beta_f32[:, j : j + 1],
+                            scale=1.0,
+                        )
+                    nc.vector.tensor_tensor(out=result[:, j, :], in0=x_tile[:, j, :], in1=rnorm[:], op=ALU.mult)
+                nc.sync.dma_start(out=out_by_tile[b, :, :, cols], in_=result[:])

@@ -20,6 +20,9 @@ POSITIONS = 64 * 64
 OUT_TILES = CHANNELS // P
 N_PASS = 512
 CHUNK = 1024
+CHUNKS = BATCH * POSITIONS // CHUNK
+PAIR = 2 * CHUNK
+AHEAD = 4
 SCALAR_COLS = 640
 
 FLOPS = 2 * CHANNELS * CHANNELS * BATCH * POSITIONS
@@ -27,17 +30,88 @@ FLOPS = 2 * CHANNELS * CHANNELS * BATCH * POSITIONS
 
 def tile_gdn_kernel(tc, x, beta, gamma_words, gamma_scales, out):
     nc = tc.nc
-    x_by_word = x.rearrange("b (p t) h w -> b p t (h w)", t=PACK)
-    x_by_tile = x.rearrange("b (j m) h w -> b m j (h w)", m=P)
-    out_by_tile = out.rearrange("b (j m) h w -> b m j (h w)", m=P)
+    x_by_word = x.rearrange("b (p t) h w -> p t b (h w)", t=PACK)
+    x_by_tile = x.rearrange("b (j m) h w -> m j b (h w)", m=P)
+    out_by_tile = out.rearrange("b (j m) h w -> m j b (h w)", m=P)
 
     with ExitStack() as ctx:
         const = ctx.enter_context(tc.tile_pool(name="const", bufs=1))
-        loads = ctx.enter_context(tc.tile_pool(name="loads", bufs=4))
+        word_pool = ctx.enter_context(tc.tile_pool(name="word_pool", bufs=AHEAD))
+        tile_pool = ctx.enter_context(tc.tile_pool(name="tile_pool", bufs=AHEAD // 2 + 1))
         quant = ctx.enter_context(tc.tile_pool(name="quant", bufs=2))
-        norms = ctx.enter_context(tc.tile_pool(name="norms", bufs=4))
-        stores = ctx.enter_context(tc.tile_pool(name="stores", bufs=3))
+        norms = ctx.enter_context(tc.tile_pool(name="norms", bufs=3))
+        stores = ctx.enter_context(tc.tile_pool(name="stores", bufs=12))
         psum = ctx.enter_context(tc.psum_pool(name="psum", bufs=8))
+        ctx.enter_context(tc.manual_schedule())
+
+        x_word = {}
+        x_tile = {}
+        codes = {}
+        scales = {}
+
+        def where(first):
+            return first // POSITIONS, first % POSITIONS
+
+        def load_by_word(k):
+            b, n0 = where(k * CHUNK)
+            x_word[k] = word_pool.tile([P, PACK, CHUNK], BF16, name="x_word")
+            nc.sync.dma_start(out=x_word[k][:], in_=x_by_word[:, :, b, n0 : n0 + CHUNK])
+
+        def load_by_tile(q):
+            b, n0 = where(q * PAIR)
+            x_tile[q] = tile_pool.tile([P, OUT_TILES, PAIR], BF16, name="x_tile")
+            nc.sync.dma_start(out=x_tile[q][:], in_=x_by_tile[:, :, b, n0 : n0 + PAIR])
+
+        def load(k):
+            load_by_word(k)
+            if k % 2 == 0:
+                load_by_tile(k // 2)
+
+        def square_and_quantise(k):
+            squares = quant.tile([P, CHUNK, PACK], BF16, align_bytes=64)
+            src = x_word[k][:].rearrange("p t (c i) -> p c t i", i=4)
+            dst = squares[:].rearrange("p (c i) t -> p c t i", i=4)
+            cut = SCALAR_COLS // 4
+            nc.scalar.activation(out=dst[:, :cut], in_=src[:, :cut], func=ACT.Square)
+            nc.vector.tensor_tensor(out=dst[:, cut:], in0=src[:, cut:], in1=src[:, cut:], op=ALU.mult)
+            codes[k] = quant.tile([P, CHUNK], U32, align_bytes=64, name="codes")
+            scales[k] = quant.tile([P, CHUNK], U8, align_bytes=64, name="scales")
+            nc.vector.quantize_mx(
+                out=codes[k][:].bitcast(FP8X4),
+                scales=scales[k][:],
+                in_=squares[:].rearrange("p c t -> p (c t)"),
+            )
+
+        def normalise(k):
+            b, n0 = where(k * CHUNK)
+            half = (k % 2) * CHUNK
+            for j in range(OUT_TILES):
+                rnorm = norms.tile([P, CHUNK], F32)
+                for c0 in range(0, CHUNK, N_PASS):
+                    mix = psum.tile([P, N_PASS], F32)
+                    nc.tensor.matmul_mx(
+                        out=mix[:],
+                        lhsT=g_words[:, 2 * P * j : 2 * P * (j + 1)].bitcast(FP4X4),
+                        lhsT_scale=g_scales[:, P * j : P * (j + 1)],
+                        rhs=codes[k][:, c0 : c0 + N_PASS].bitcast(FP8X4),
+                        rhs_scale=scales[k][:, c0 : c0 + N_PASS],
+                        start=True,
+                        stop=True,
+                    )
+                    nc.scalar.activation(
+                        out=rnorm[:, c0 : c0 + N_PASS],
+                        in_=mix[:],
+                        func=ACT.Abs_reciprocal_sqrt,
+                        bias=beta_f32[:, j : j + 1],
+                        scale=1.0,
+                    )
+                result = stores.tile([P, CHUNK], F32)
+                nc.vector.tensor_tensor(
+                    out=result[:], in0=x_tile[k // 2][:, j, half : half + CHUNK], in1=rnorm[:], op=ALU.mult
+                )
+                nc.sync.dma_start(out=out_by_tile[:, j, b, n0 : n0 + CHUNK], in_=result[:])
+
+        load_by_word(0)
 
         g_words = const.tile([P, 2 * CHANNELS], U8, align_bytes=64)
         g_scales = const.tile([P, CHANNELS], U8, align_bytes=64)
@@ -55,49 +129,13 @@ def tile_gdn_kernel(tc, x, beta, gamma_words, gamma_scales, out):
         beta_f32 = const.tile([P, OUT_TILES], F32)
         nc.vector.tensor_copy(out=beta_f32[:], in_=beta_bf16[:])
 
-        for b in range(BATCH):
-            for first in range(0, POSITIONS, CHUNK):
-                cols = slice(first, first + CHUNK)
-                x_word = loads.tile([P, PACK, CHUNK], BF16)
-                nc.sync.dma_start(out=x_word[:], in_=x_by_word[b, :, :, cols])
-                x_tile = loads.tile([P, OUT_TILES, CHUNK], BF16)
-                nc.sync.dma_start(out=x_tile[:], in_=x_by_tile[b, :, :, cols])
-
-                squares = quant.tile([P, CHUNK, PACK], BF16, align_bytes=64)
-                src = x_word[:].rearrange("p t (c i) -> p c t i", i=4)
-                dst = squares[:].rearrange("p (c i) t -> p c t i", i=4)
-                cut = SCALAR_COLS // 4
-                nc.scalar.activation(out=dst[:, :cut], in_=src[:, :cut], func=ACT.Square)
-                nc.vector.tensor_tensor(out=dst[:, cut:], in0=src[:, cut:], in1=src[:, cut:], op=ALU.mult)
-
-                codes = quant.tile([P, CHUNK], U32, align_bytes=64)
-                scales = quant.tile([P, CHUNK], U8, align_bytes=64)
-                nc.vector.quantize_mx(
-                    out=codes[:].bitcast(FP8X4),
-                    scales=scales[:],
-                    in_=squares[:].rearrange("p c t -> p (c t)"),
-                )
-
-                result = stores.tile([P, OUT_TILES, CHUNK], F32)
-                for j in range(OUT_TILES):
-                    rnorm = norms.tile([P, CHUNK], F32)
-                    for n0 in range(0, CHUNK, N_PASS):
-                        mix = psum.tile([P, N_PASS], F32)
-                        nc.tensor.matmul_mx(
-                            out=mix[:],
-                            lhsT=g_words[:, 2 * P * j : 2 * P * (j + 1)].bitcast(FP4X4),
-                            lhsT_scale=g_scales[:, P * j : P * (j + 1)],
-                            rhs=codes[:, n0 : n0 + N_PASS].bitcast(FP8X4),
-                            rhs_scale=scales[:, n0 : n0 + N_PASS],
-                            start=True,
-                            stop=True,
-                        )
-                        nc.scalar.activation(
-                            out=rnorm[:, n0 : n0 + N_PASS],
-                            in_=mix[:],
-                            func=ACT.Abs_reciprocal_sqrt,
-                            bias=beta_f32[:, j : j + 1],
-                            scale=1.0,
-                        )
-                    nc.vector.tensor_tensor(out=result[:, j, :], in0=x_tile[:, j, :], in1=rnorm[:], op=ALU.mult)
-                nc.sync.dma_start(out=out_by_tile[b, :, :, cols], in_=result[:])
+        load_by_tile(0)
+        for k in range(1, AHEAD):
+            load(k)
+        square_and_quantise(0)
+        for k in range(CHUNKS):
+            if k + AHEAD < CHUNKS:
+                load(k + AHEAD)
+            if k + 1 < CHUNKS:
+                square_and_quantise(k + 1)
+            normalise(k)

@@ -40,7 +40,7 @@ def tile_gdn_kernel(tc, x, beta, gamma_words, gamma_scales, out):
         tile_pool = ctx.enter_context(tc.tile_pool(name="tile_pool", bufs=AHEAD // 2 + 1))
         quant = ctx.enter_context(tc.tile_pool(name="quant", bufs=2))
         norms = ctx.enter_context(tc.tile_pool(name="norms", bufs=3))
-        stores = ctx.enter_context(tc.tile_pool(name="stores", bufs=12))
+        stores = ctx.enter_context(tc.tile_pool(name="stores", bufs=24))
         psum = ctx.enter_context(tc.psum_pool(name="psum", bufs=8))
         ctx.enter_context(tc.manual_schedule())
 
@@ -64,7 +64,7 @@ def tile_gdn_kernel(tc, x, beta, gamma_words, gamma_scales, out):
 
         def load(k):
             load_by_word(k)
-            if k % 2 == 0:
+            if k % 2 == 1:
                 load_by_tile(k // 2)
 
         def square_and_quantise(k):
@@ -113,6 +113,10 @@ def tile_gdn_kernel(tc, x, beta, gamma_words, gamma_scales, out):
 
         load_by_word(0)
 
+        one = const.tile([P, 1], F32)
+        nc.vector.memset(one[:], 1.0)
+        nc.scalar.activation(out=one[:], in_=one[:], func=ACT.Abs_reciprocal_sqrt)
+
         g_words = const.tile([P, 2 * CHANNELS], U8, align_bytes=64)
         g_scales = const.tile([P, CHANNELS], U8, align_bytes=64)
         nc.vector.memset(g_scales[:].bitcast(I32), 0)
@@ -129,7 +133,6 @@ def tile_gdn_kernel(tc, x, beta, gamma_words, gamma_scales, out):
         beta_f32 = const.tile([P, OUT_TILES], F32)
         nc.vector.tensor_copy(out=beta_f32[:], in_=beta_bf16[:])
 
-        load_by_tile(0)
         for k in range(1, AHEAD):
             load(k)
         square_and_quantise(0)

@@ -20,9 +20,8 @@ POSITIONS = 64 * 64
 OUT_TILES = CHANNELS // P
 N_PASS = 512
 CHUNK = 1024
-CHUNKS = BATCH * POSITIONS // CHUNK
-PAIR = 2 * CHUNK
-AHEAD = 4
+CHUNKS = POSITIONS // CHUNK
+STORE = 2048
 SCALAR_COLS = 640
 
 FLOPS = 2 * CHANNELS * CHANNELS * BATCH * POSITIONS
@@ -30,17 +29,18 @@ FLOPS = 2 * CHANNELS * CHANNELS * BATCH * POSITIONS
 
 def tile_gdn_kernel(tc, x, beta, gamma_words, gamma_scales, out):
     nc = tc.nc
-    x_by_word = x.rearrange("b (p t) h w -> p t b (h w)", t=PACK)
-    x_by_tile = x.rearrange("b (j m) h w -> m j b (h w)", m=P)
-    out_by_tile = out.rearrange("b (j m) h w -> m j b (h w)", m=P)
+    x_by_word = x.rearrange("b (p t) h w -> b p t (h w)", t=PACK)
+    x_by_tile = x.rearrange("b (j m) h w -> b j m (h w)", m=P)
+    out_by_tile = out.rearrange("b (j m) h w -> b j m (h w)", m=P)
 
     with ExitStack() as ctx:
         const = ctx.enter_context(tc.tile_pool(name="const", bufs=1))
-        word_pool = ctx.enter_context(tc.tile_pool(name="word_pool", bufs=AHEAD))
-        tile_pool = ctx.enter_context(tc.tile_pool(name="tile_pool", bufs=AHEAD // 2 + 1))
-        quant = ctx.enter_context(tc.tile_pool(name="quant", bufs=2))
+        word_pool = ctx.enter_context(tc.tile_pool(name="word_pool", bufs=1))
+        tile_pool = ctx.enter_context(tc.tile_pool(name="tile_pool", bufs=OUT_TILES + 2))
+        square_pool = ctx.enter_context(tc.tile_pool(name="square_pool", bufs=2))
+        code_pool = ctx.enter_context(tc.tile_pool(name="code_pool", bufs=CHUNKS))
         norms = ctx.enter_context(tc.tile_pool(name="norms", bufs=3))
-        stores = ctx.enter_context(tc.tile_pool(name="stores", bufs=24))
+        stores = ctx.enter_context(tc.tile_pool(name="stores", bufs=8))
         psum = ctx.enter_context(tc.psum_pool(name="psum", bufs=8))
         ctx.enter_context(tc.manual_schedule())
 
@@ -49,73 +49,66 @@ def tile_gdn_kernel(tc, x, beta, gamma_words, gamma_scales, out):
         codes = {}
         scales = {}
 
-        def where(first):
-            return first // POSITIONS, first % POSITIONS
+        def load_by_word(b, pieces):
+            width = POSITIONS // pieces
+            for n0 in range(0, POSITIONS, width):
+                piece = word_pool.tile([P, PACK, width], BF16, name="x_word_%d_%d" % (b, n0))
+                nc.sync.dma_start(out=piece[:], in_=x_by_word[b, :, :, n0 : n0 + width])
+                for c0 in range(0, width, CHUNK):
+                    x_word[b, (n0 + c0) // CHUNK] = piece[:, :, c0 : c0 + CHUNK]
 
-        def load_by_word(k):
-            b, n0 = where(k * CHUNK)
-            x_word[k] = word_pool.tile([P, PACK, CHUNK], BF16, name="x_word")
-            nc.sync.dma_start(out=x_word[k][:], in_=x_by_word[:, :, b, n0 : n0 + CHUNK])
+        def load_by_tile(b, j):
+            x_tile[b, j] = tile_pool.tile([P, POSITIONS], BF16, name="x_tile")
+            nc.sync.dma_start(out=x_tile[b, j][:], in_=x_by_tile[b, j])
 
-        def load_by_tile(q):
-            b, n0 = where(q * PAIR)
-            x_tile[q] = tile_pool.tile([P, OUT_TILES, PAIR], BF16, name="x_tile")
-            nc.sync.dma_start(out=x_tile[q][:], in_=x_by_tile[:, :, b, n0 : n0 + PAIR])
-
-        def load(k):
-            load_by_word(k)
-            if k % 2 == 1:
-                load_by_tile(k // 2)
-
-        def square_and_quantise(k):
-            squares = quant.tile([P, CHUNK, PACK], BF16, align_bytes=64)
-            src = x_word[k][:].rearrange("p t (c i) -> p c t i", i=4)
+        def square_and_quantise(b, c):
+            squares = square_pool.tile([P, CHUNK, PACK], BF16, align_bytes=64)
+            src = x_word[b, c].rearrange("p t (c i) -> p c t i", i=4)
             dst = squares[:].rearrange("p (c i) t -> p c t i", i=4)
             cut = SCALAR_COLS // 4
             nc.scalar.activation(out=dst[:, :cut], in_=src[:, :cut], func=ACT.Square)
             nc.vector.tensor_tensor(out=dst[:, cut:], in0=src[:, cut:], in1=src[:, cut:], op=ALU.mult)
-            codes[k] = quant.tile([P, CHUNK], U32, align_bytes=64, name="codes")
-            scales[k] = quant.tile([P, CHUNK], U8, align_bytes=64, name="scales")
+            codes[b, c] = code_pool.tile([P, CHUNK], U32, align_bytes=64, name="codes")
+            scales[b, c] = code_pool.tile([P, CHUNK], U8, align_bytes=64, name="scales")
             nc.vector.quantize_mx(
-                out=codes[k][:].bitcast(FP8X4),
-                scales=scales[k][:],
+                out=codes[b, c][:].bitcast(FP8X4),
+                scales=scales[b, c][:],
                 in_=squares[:].rearrange("p c t -> p (c t)"),
             )
 
-        def normalise(k):
-            b, n0 = where(k * CHUNK)
-            half = (k % 2) * CHUNK
-            for j in range(OUT_TILES):
-                rnorm = norms.tile([P, CHUNK], F32)
-                for c0 in range(0, CHUNK, N_PASS):
-                    mix = psum.tile([P, N_PASS], F32)
-                    nc.tensor.matmul_mx(
-                        out=mix[:],
-                        lhsT=g_words[:, 2 * P * j : 2 * P * (j + 1)].bitcast(FP4X4),
-                        lhsT_scale=g_scales[:, P * j : P * (j + 1)],
-                        rhs=codes[k][:, c0 : c0 + N_PASS].bitcast(FP8X4),
-                        rhs_scale=scales[k][:, c0 : c0 + N_PASS],
-                        start=True,
-                        stop=True,
+        def normalise(b, j):
+            for s0 in range(0, POSITIONS, STORE):
+                result = stores.tile([P, STORE], F32)
+                for r0 in range(0, STORE, CHUNK):
+                    c = (s0 + r0) // CHUNK
+                    rnorm = norms.tile([P, CHUNK], F32)
+                    for c0 in range(0, CHUNK, N_PASS):
+                        mix = psum.tile([P, N_PASS], F32)
+                        nc.tensor.matmul_mx(
+                            out=mix[:],
+                            lhsT=g_words[:, 2 * P * j : 2 * P * (j + 1)].bitcast(FP4X4),
+                            lhsT_scale=g_scales[:, P * j : P * (j + 1)],
+                            rhs=codes[b, c][:, c0 : c0 + N_PASS].bitcast(FP8X4),
+                            rhs_scale=scales[b, c][:, c0 : c0 + N_PASS],
+                            start=True,
+                            stop=True,
+                        )
+                        nc.scalar.activation(
+                            out=rnorm[:, c0 : c0 + N_PASS],
+                            in_=mix[:],
+                            func=ACT.Abs_reciprocal_sqrt,
+                            bias=beta_f32[:, j : j + 1],
+                            scale=1.0,
+                        )
+                    nc.vector.tensor_tensor(
+                        out=result[:, r0 : r0 + CHUNK],
+                        in0=x_tile[b, j][:, s0 + r0 : s0 + r0 + CHUNK],
+                        in1=rnorm[:],
+                        op=ALU.mult,
                     )
-                    nc.scalar.activation(
-                        out=rnorm[:, c0 : c0 + N_PASS],
-                        in_=mix[:],
-                        func=ACT.Abs_reciprocal_sqrt,
-                        bias=beta_f32[:, j : j + 1],
-                        scale=1.0,
-                    )
-                result = stores.tile([P, CHUNK], F32)
-                nc.vector.tensor_tensor(
-                    out=result[:], in0=x_tile[k // 2][:, j, half : half + CHUNK], in1=rnorm[:], op=ALU.mult
-                )
-                nc.sync.dma_start(out=out_by_tile[:, j, b, n0 : n0 + CHUNK], in_=result[:])
+                nc.sync.dma_start(out=out_by_tile[b, j, :, s0 : s0 + STORE], in_=result[:])
 
-        load_by_word(0)
-
-        one = const.tile([P, 1], F32)
-        nc.vector.memset(one[:], 1.0)
-        nc.scalar.activation(out=one[:], in_=one[:], func=ACT.Abs_reciprocal_sqrt)
+        load_by_word(0, CHUNKS)
 
         g_words = const.tile([P, 2 * CHANNELS], U8, align_bytes=64)
         g_scales = const.tile([P, CHANNELS], U8, align_bytes=64)
@@ -133,12 +126,18 @@ def tile_gdn_kernel(tc, x, beta, gamma_words, gamma_scales, out):
         beta_f32 = const.tile([P, OUT_TILES], F32)
         nc.vector.tensor_copy(out=beta_f32[:], in_=beta_bf16[:])
 
-        for k in range(1, AHEAD):
-            load(k)
-        square_and_quantise(0)
-        for k in range(CHUNKS):
-            if k + AHEAD < CHUNKS:
-                load(k + AHEAD)
-            if k + 1 < CHUNKS:
-                square_and_quantise(k + 1)
-            normalise(k)
+        one = const.tile([P, 1], F32)
+        nc.vector.memset(one[:], 1.0)
+        nc.scalar.activation(out=one[:], in_=one[:], func=ACT.Abs_reciprocal_sqrt)
+
+        for j in range(OUT_TILES):
+            load_by_tile(0, j)
+        for b in range(BATCH):
+            if b + 1 < BATCH:
+                load_by_word(b + 1, 1)
+            for c in range(CHUNKS):
+                square_and_quantise(b, c)
+            for j in range(OUT_TILES):
+                if b + 1 < BATCH:
+                    load_by_tile(b + 1, j)
+                normalise(b, j)

@@ -17,12 +17,9 @@ PACK = 4
 BATCH = 2
 CHANNELS = 512
 POSITIONS = 64 * 64
-OUT_TILES = CHANNELS // P
 N_PASS = 512
-CHUNK = 1024
-CHUNKS = POSITIONS // CHUNK
-STORE = 2048
-SCALAR_COLS = 640
+CHUNK_WIDTHS = ((512, 512, 1024, 1024, 1024), (1024, 1024, 1024, 512, 512))
+SCALAR_SHARE = (21, 32)
 
 FLOPS = 2 * CHANNELS * CHANNELS * BATCH * POSITIONS
 
@@ -30,114 +27,135 @@ FLOPS = 2 * CHANNELS * CHANNELS * BATCH * POSITIONS
 def tile_gdn_kernel(tc, x, beta, gamma_words, gamma_scales, out):
     nc = tc.nc
     x_by_word = x.rearrange("b (p t) h w -> b p t (h w)", t=PACK)
-    x_by_tile = x.rearrange("b (j m) h w -> b j m (h w)", m=P)
-    out_by_tile = out.rearrange("b (j m) h w -> b j m (h w)", m=P)
+    out_by_word = out.rearrange("b (p t) h w -> b p t (h w)", t=PACK)
+    chunks = []
+    for b in range(BATCH):
+        assert sum(CHUNK_WIDTHS[b]) == POSITIONS
+        for i, width in enumerate(CHUNK_WIDTHS[b]):
+            chunks.append((b, sum(CHUNK_WIDTHS[b][:i]), width))
+    last = len(chunks) - 1
 
     with ExitStack() as ctx:
         const = ctx.enter_context(tc.tile_pool(name="const", bufs=1))
         word_pool = ctx.enter_context(tc.tile_pool(name="word_pool", bufs=1))
-        tile_pool = ctx.enter_context(tc.tile_pool(name="tile_pool", bufs=OUT_TILES + 2))
-        square_pool = ctx.enter_context(tc.tile_pool(name="square_pool", bufs=2))
-        code_pool = ctx.enter_context(tc.tile_pool(name="code_pool", bufs=CHUNKS))
-        norms = ctx.enter_context(tc.tile_pool(name="norms", bufs=3))
-        stores = ctx.enter_context(tc.tile_pool(name="stores", bufs=8))
+        square_pool = ctx.enter_context(tc.tile_pool(name="square_pool", bufs=3))
+        code_pool = ctx.enter_context(tc.tile_pool(name="code_pool", bufs=3))
+        norms = ctx.enter_context(tc.tile_pool(name="norms", bufs=6))
+        stores = ctx.enter_context(tc.tile_pool(name="stores", bufs=12))
         psum = ctx.enter_context(tc.psum_pool(name="psum", bufs=8))
         ctx.enter_context(tc.manual_schedule())
 
         x_word = {}
-        x_tile = {}
+        squares = {}
         codes = {}
         scales = {}
+        mixes = {}
+        rnorms = {}
 
-        def load_by_word(b, pieces):
-            width = POSITIONS // pieces
-            for n0 in range(0, POSITIONS, width):
-                piece = word_pool.tile([P, PACK, width], BF16, name="x_word_%d_%d" % (b, n0))
-                nc.sync.dma_start(out=piece[:], in_=x_by_word[b, :, :, n0 : n0 + width])
-                for c0 in range(0, width, CHUNK):
-                    x_word[b, (n0 + c0) // CHUNK] = piece[:, :, c0 : c0 + CHUNK]
+        def load(k):
+            b, n0, width = chunks[k]
+            x_word[k] = word_pool.tile([P, PACK, width], BF16, name="x_word_%d" % k)
+            nc.sync.dma_start(out=x_word[k][:], in_=x_by_word[b, :, :, n0 : n0 + width])
 
-        def load_by_tile(b, j):
-            x_tile[b, j] = tile_pool.tile([P, POSITIONS], BF16, name="x_tile")
-            nc.sync.dma_start(out=x_tile[b, j][:], in_=x_by_tile[b, j])
-
-        def square_and_quantise(b, c):
-            squares = square_pool.tile([P, CHUNK, PACK], BF16, align_bytes=64)
-            src = x_word[b, c].rearrange("p t (c i) -> p c t i", i=4)
-            dst = squares[:].rearrange("p (c i) t -> p c t i", i=4)
-            cut = SCALAR_COLS // 4
+        def square(k):
+            width = chunks[k][2]
+            squares[k] = square_pool.tile([P, width, PACK], BF16, align_bytes=64, name="squares")
+            src = x_word[k][:].rearrange("p t (c i) -> p c t i", i=4)
+            dst = squares[k][:].rearrange("p (c i) t -> p c t i", i=4)
+            cut = width * SCALAR_SHARE[0] // SCALAR_SHARE[1] // 4
             nc.scalar.activation(out=dst[:, :cut], in_=src[:, :cut], func=ACT.Square)
             nc.vector.tensor_tensor(out=dst[:, cut:], in0=src[:, cut:], in1=src[:, cut:], op=ALU.mult)
-            codes[b, c] = code_pool.tile([P, CHUNK], U32, align_bytes=64, name="codes")
-            scales[b, c] = code_pool.tile([P, CHUNK], U8, align_bytes=64, name="scales")
+
+        def quantise(k):
+            width = chunks[k][2]
+            codes[k] = code_pool.tile([P, width], U32, align_bytes=64, name="codes")
+            scales[k] = code_pool.tile([P, width], U8, align_bytes=64, name="scales")
             nc.vector.quantize_mx(
-                out=codes[b, c][:].bitcast(FP8X4),
-                scales=scales[b, c][:],
-                in_=squares[:].rearrange("p c t -> p (c t)"),
+                out=codes[k][:].bitcast(FP8X4),
+                scales=scales[k][:],
+                in_=squares[k][:].rearrange("p c t -> p (c t)"),
             )
 
-        def normalise(b, j):
-            for s0 in range(0, POSITIONS, STORE):
-                result = stores.tile([P, STORE], F32)
-                for r0 in range(0, STORE, CHUNK):
-                    c = (s0 + r0) // CHUNK
-                    rnorm = norms.tile([P, CHUNK], F32)
-                    for c0 in range(0, CHUNK, N_PASS):
-                        mix = psum.tile([P, N_PASS], F32)
-                        nc.tensor.matmul_mx(
-                            out=mix[:],
-                            lhsT=g_words[:, 2 * P * j : 2 * P * (j + 1)].bitcast(FP4X4),
-                            lhsT_scale=g_scales[:, P * j : P * (j + 1)],
-                            rhs=codes[b, c][:, c0 : c0 + N_PASS].bitcast(FP8X4),
-                            rhs_scale=scales[b, c][:, c0 : c0 + N_PASS],
-                            start=True,
-                            stop=True,
-                        )
-                        nc.scalar.activation(
-                            out=rnorm[:, c0 : c0 + N_PASS],
-                            in_=mix[:],
-                            func=ACT.Abs_reciprocal_sqrt,
-                            bias=beta_f32[:, j : j + 1],
-                            scale=1.0,
-                        )
-                    nc.vector.tensor_tensor(
-                        out=result[:, r0 : r0 + CHUNK],
-                        in0=x_tile[b, j][:, s0 + r0 : s0 + r0 + CHUNK],
-                        in1=rnorm[:],
-                        op=ALU.mult,
+        def multiply_mx(k):
+            for t in range(PACK):
+                for h in range(chunks[k][2] // N_PASS):
+                    mixes[k, t, h] = psum.tile([P, N_PASS], F32, name="mix")
+                    nc.tensor.matmul_mx(
+                        out=mixes[k, t, h][:],
+                        lhsT=g_words[:, 2 * P * t : 2 * P * (t + 1)].bitcast(FP4X4),
+                        lhsT_scale=g_scales[:, P * t : P * (t + 1)],
+                        rhs=codes[k][:, N_PASS * h : N_PASS * (h + 1)].bitcast(FP8X4),
+                        rhs_scale=scales[k][:, N_PASS * h : N_PASS * (h + 1)],
+                        start=True,
+                        stop=True,
                     )
-                nc.sync.dma_start(out=out_by_tile[b, j, :, s0 : s0 + STORE], in_=result[:])
 
-        load_by_word(0, CHUNKS)
+        def reciprocal_root(k, t):
+            rnorms[k, t] = norms.tile([P, chunks[k][2]], F32, name="rnorm")
+            for h in range(chunks[k][2] // N_PASS):
+                nc.scalar.activation(
+                    out=rnorms[k, t][:, N_PASS * h : N_PASS * (h + 1)],
+                    in_=mixes[k, t, h][:],
+                    func=ACT.Abs_reciprocal_sqrt,
+                    bias=beta_f32[:, t : t + 1],
+                    scale=1.0,
+                )
 
-        g_words = const.tile([P, 2 * CHANNELS], U8, align_bytes=64)
-        g_scales = const.tile([P, CHANNELS], U8, align_bytes=64)
-        nc.vector.memset(g_scales[:].bitcast(I32), 0)
-        nc.sync.dma_start(out=g_words[:].bitcast(I32), in_=gamma_words[0].bitcast(I32))
+        def normalise(k, t):
+            b, n0, width = chunks[k]
+            result = stores.tile([P, width], F32, name="result")
+            nc.vector.tensor_tensor(out=result[:], in0=x_word[k][:, t, :], in1=rnorms[k, t][:], op=ALU.mult)
+            nc.sync.dma_start(out=out_by_word[b, :, t, n0 : n0 + width], in_=result[:])
+
+        load(0)
+        g_words_raw = const.tile([P, 2 * CHANNELS], U8, align_bytes=64)
+        g_scales_raw = const.tile([P, CHANNELS], U8, align_bytes=64)
+        nc.vector.memset(g_scales_raw[:].bitcast(I32), 0)
+        nc.sync.dma_start(out=g_words_raw[:].bitcast(I32), in_=gamma_words[0].bitcast(I32))
         for quadrant in range(4):
             nc.sync.dma_start(
-                out=g_scales[32 * quadrant : 32 * quadrant + 4, :].bitcast(I32),
+                out=g_scales_raw[32 * quadrant : 32 * quadrant + 4, :].bitcast(I32),
                 in_=gamma_scales[0, 4 * quadrant : 4 * quadrant + 4, :].bitcast(I32),
             )
+        for k in range(1, len(chunks)):
+            load(k)
 
-        beta_bf16 = const.tile([P, OUT_TILES], BF16)
-        with nc.allow_non_contiguous_dma(reason="512 single elements, once"):
-            nc.scalar.dma_start(out=beta_bf16[:], in_=beta.rearrange("a (j m) h w -> m (a j h w)", m=P))
-        beta_f32 = const.tile([P, OUT_TILES], F32)
+        beta_bf16 = const.tile([P, PACK], BF16)
+        nc.scalar.dma_start(out=beta_bf16[:], in_=beta.rearrange("a (p t) h w -> p (a t h w)", t=PACK))
+        beta_f32 = const.tile([P, PACK], F32)
         nc.vector.tensor_copy(out=beta_f32[:], in_=beta_bf16[:])
 
         one = const.tile([P, 1], F32)
         nc.vector.memset(one[:], 1.0)
         nc.scalar.activation(out=one[:], in_=one[:], func=ACT.Abs_reciprocal_sqrt)
 
-        for j in range(OUT_TILES):
-            load_by_tile(0, j)
-        for b in range(BATCH):
-            if b + 1 < BATCH:
-                load_by_word(b + 1, 1)
-            for c in range(CHUNKS):
-                square_and_quantise(b, c)
-            for j in range(OUT_TILES):
-                if b + 1 < BATCH:
-                    load_by_tile(b + 1, j)
-                normalise(b, j)
+        square(0)
+
+        g_words = const.tile([P, 2 * CHANNELS], U8, align_bytes=64)
+        g_scales = const.tile([P, CHANNELS], U8, align_bytes=64)
+        nc.vector.tensor_copy(
+            out=g_words[:].rearrange("p (t m e) -> p m t e", t=PACK, e=2),
+            in_=g_words_raw[:].rearrange("p (m t e) -> p m t e", t=PACK, e=2),
+        )
+        nc.vector.tensor_copy(
+            out=g_scales[:].rearrange("p (t m) -> p m t", t=PACK),
+            in_=g_scales_raw[:].rearrange("p (m t) -> p m t", t=PACK),
+        )
+
+        quantise(0)
+        multiply_mx(0)
+        for k in range(len(chunks)):
+            if k < last:
+                square(k + 1)
+            if k > 0:
+                normalise(k - 1, 2)
+                normalise(k - 1, 3)
+            for t in range(PACK):
+                reciprocal_root(k, t)
+            if k < last:
+                quantise(k + 1)
+                multiply_mx(k + 1)
+            normalise(k, 0)
+            normalise(k, 1)
+        normalise(last, 2)
+        normalise(last, 3)

@@ -19,7 +19,7 @@ CHANNELS = 512
 POSITIONS = 64 * 64
 N_PASS = 512
 CHUNK_WIDTHS = ((512, 512, 1024, 1024, 1024), (1024, 1024, 1024, 512, 512))
-SCALAR_SHARE = (21, 32)
+SCALAR_SHARE = (19, 32)
 
 FLOPS = 2 * CHANNELS * CHANNELS * BATCH * POSITIONS
 

@@ -19,7 +19,7 @@ CHANNELS = 512
 POSITIONS = 64 * 64
 N_PASS = 512
 CHUNK_WIDTHS = ((512, 512, 1024, 1024, 1024), (1024, 1024, 1024, 512, 512))
-SCALAR_SHARE = (19, 32)
+SCALAR_SHARE = (5, 8)
 
 FLOPS = 2 * CHANNELS * CHANNELS * BATCH * POSITIONS
 

@@ -133,14 +133,15 @@ def tile_gdn_kernel(tc, x, beta, gamma_words, gamma_scales, out):
 
         g_words = const.tile([P, 2 * CHANNELS], U8, align_bytes=64)
         g_scales = const.tile([P, CHANNELS], U8, align_bytes=64)
-        nc.vector.tensor_copy(
-            out=g_words[:].rearrange("p (t m e) -> p m t e", t=PACK, e=2),
-            in_=g_words_raw[:].rearrange("p (m t e) -> p m t e", t=PACK, e=2),
-        )
-        nc.vector.tensor_copy(
-            out=g_scales[:].rearrange("p (t m) -> p m t", t=PACK),
-            in_=g_scales_raw[:].rearrange("p (m t) -> p m t", t=PACK),
-        )
+        for t in range(PACK):
+            nc.vector.tensor_copy(
+                out=g_words[:, 2 * P * t : 2 * P * (t + 1)].rearrange("p (m e) -> p m e", e=2),
+                in_=g_words_raw[:].rearrange("p (m t e) -> p t m e", t=PACK, e=2)[:, t],
+            )
+            nc.vector.tensor_copy(
+                out=g_scales[:, P * t : P * (t + 1)],
+                in_=g_scales_raw[:].rearrange("p (m t) -> p t m", t=PACK)[:, t],
+            )
 
         quantise(0)
         multiply_mx(0)

@@ -19,6 +19,7 @@ CHANNELS = 512
 POSITIONS = 64 * 64
 N_PASS = 512
 CHUNK_WIDTHS = ((512, 512, 1024, 1024, 1024), (1024, 1024, 1024, 512, 512))
+RUN = 8
 SCALAR_SHARE = (5, 8)
 
 FLOPS = 2 * CHANNELS * CHANNELS * BATCH * POSITIONS
@@ -60,9 +61,9 @@ def tile_gdn_kernel(tc, x, beta, gamma_words, gamma_scales, out):
         def square(k):
             width = chunks[k][2]
             squares[k] = square_pool.tile([P, width, PACK], BF16, align_bytes=64, name="squares")
-            src = x_word[k][:].rearrange("p t (c i) -> p c t i", i=4)
-            dst = squares[k][:].rearrange("p (c i) t -> p c t i", i=4)
-            cut = width * SCALAR_SHARE[0] // SCALAR_SHARE[1] // 4
+            src = x_word[k][:].rearrange("p t (c i) -> p c t i", i=RUN)
+            dst = squares[k][:].rearrange("p (c i) t -> p c t i", i=RUN)
+            cut = width * SCALAR_SHARE[0] // SCALAR_SHARE[1] // RUN
             nc.scalar.activation(out=dst[:, :cut], in_=src[:, :cut], func=ACT.Square)
             nc.vector.tensor_tensor(out=dst[:, cut:], in0=src[:, cut:], in1=src[:, cut:], op=ALU.mult)
 

@@ -21,6 +21,7 @@ N_PASS = 512
 CHUNK_WIDTHS = ((512, 512, 1024, 1024, 1024), (1024, 1024, 1024, 512, 512))
 RUN = 8
 SCALAR_SHARE = (5, 8)
+LAST_SHARES = ((3, 4), (1, 1))
 
 FLOPS = 2 * CHANNELS * CHANNELS * BATCH * POSITIONS
 
@@ -63,9 +64,12 @@ def tile_gdn_kernel(tc, x, beta, gamma_words, gamma_scales, out):
             squares[k] = square_pool.tile([P, width, PACK], BF16, align_bytes=64, name="squares")
             src = x_word[k][:].rearrange("p t (c i) -> p c t i", i=RUN)
             dst = squares[k][:].rearrange("p (c i) t -> p c t i", i=RUN)
-            cut = width * SCALAR_SHARE[0] // SCALAR_SHARE[1] // RUN
+            from_end = last - k
+            share = LAST_SHARES[-1 - from_end] if from_end < len(LAST_SHARES) else SCALAR_SHARE
+            cut = width * share[0] // share[1] // RUN
             nc.scalar.activation(out=dst[:, :cut], in_=src[:, :cut], func=ACT.Square)
-            nc.vector.tensor_tensor(out=dst[:, cut:], in0=src[:, cut:], in1=src[:, cut:], op=ALU.mult)
+            if cut < width // RUN:
+                nc.vector.tensor_tensor(out=dst[:, cut:], in0=src[:, cut:], in1=src[:, cut:], op=ALU.mult)
 
         def quantise(k):
             width = chunks[k][2]

@@ -1,6 +1,7 @@
 from contextlib import ExitStack
 
 import concourse.mybir as mybir
+from concourse.masks import make_identity
 
 F32 = mybir.dt.float32
 BF16 = mybir.dt.bfloat16
@@ -20,8 +21,11 @@ POSITIONS = 64 * 64
 N_PASS = 512
 CHUNK_WIDTHS = ((512, 512, 1024, 1024, 1024), (1024, 1024, 1024, 512, 512))
 RUN = 8
-SCALAR_SHARE = (5, 8)
-LAST_SHARES = ((3, 4), (1, 1))
+BLOCK = 256
+MIRRORED = (0, 0, 512, 512, 512, 512, 512, 512, 0, 0)
+VECTOR_SQUARES = (192, 192, 128, 128, 128, 128, 128, 128, 192, 192)
+POOL_PRODUCTS = (256, 256, 448, 448, 448, 448, 320, 256, 0, 0)
+AHEAD = 3
 
 FLOPS = 2 * CHANNELS * CHANNELS * BATCH * POSITIONS
 
@@ -36,18 +40,23 @@ def tile_gdn_kernel(tc, x, beta, gamma_words, gamma_scales, out):
         for i, width in enumerate(CHUNK_WIDTHS[b]):
             chunks.append((b, sum(CHUNK_WIDTHS[b][:i]), width))
     last = len(chunks) - 1
+    mirrored = [k for k in range(len(chunks)) if MIRRORED[k]]
+    first = mirrored[0]
+    streamed = mirrored[-1] + 1
 
     with ExitStack() as ctx:
         const = ctx.enter_context(tc.tile_pool(name="const", bufs=1))
         word_pool = ctx.enter_context(tc.tile_pool(name="word_pool", bufs=1))
         square_pool = ctx.enter_context(tc.tile_pool(name="square_pool", bufs=3))
         code_pool = ctx.enter_context(tc.tile_pool(name="code_pool", bufs=3))
-        norms = ctx.enter_context(tc.tile_pool(name="norms", bufs=6))
-        stores = ctx.enter_context(tc.tile_pool(name="stores", bufs=12))
-        psum = ctx.enter_context(tc.psum_pool(name="psum", bufs=8))
+        norms = ctx.enter_context(tc.tile_pool(name="norms", bufs=3))
+        stores = ctx.enter_context(tc.tile_pool(name="stores", bufs=6))
+        psum = ctx.enter_context(tc.psum_pool(name="psum", bufs=AHEAD))
+        mirrors = ctx.enter_context(tc.psum_pool(name="mirrors", bufs=5))
         ctx.enter_context(tc.manual_schedule())
 
         x_word = {}
+        x_mirror = {}
         squares = {}
         codes = {}
         scales = {}
@@ -59,17 +68,52 @@ def tile_gdn_kernel(tc, x, beta, gamma_words, gamma_scales, out):
             x_word[k] = word_pool.tile([P, PACK, width], BF16, name="x_word_%d" % k)
             nc.sync.dma_start(out=x_word[k][:], in_=x_by_word[b, :, :, n0 : n0 + width])
 
-        def square(k):
-            width = chunks[k][2]
-            squares[k] = square_pool.tile([P, width, PACK], BF16, align_bytes=64, name="squares")
+        def blocks(k):
+            return range(MIRRORED[k] // BLOCK)
+
+        def mirror(k, i):
+            x_mirror[k, i] = mirrors.tile([P, PACK, BLOCK], BF16, name="x_mirror")
+            for t in range(0, PACK, 2):
+                nc.tensor.matmul(
+                    out=x_mirror[k, i][:, t : t + 2, :],
+                    lhsT=identity[:],
+                    rhs=x_word[k][:, t : t + 2, BLOCK * i : BLOCK * (i + 1)],
+                    start=True,
+                    stop=True,
+                )
+
+        def square_views(k):
             src = x_word[k][:].rearrange("p t (c i) -> p c t i", i=RUN)
             dst = squares[k][:].rearrange("p (c i) t -> p c t i", i=RUN)
-            from_end = last - k
-            share = LAST_SHARES[-1 - from_end] if from_end < len(LAST_SHARES) else SCALAR_SHARE
-            cut = width * share[0] // share[1] // RUN
-            nc.scalar.activation(out=dst[:, :cut], in_=src[:, :cut], func=ACT.Square)
-            if cut < width // RUN:
-                nc.vector.tensor_tensor(out=dst[:, cut:], in0=src[:, cut:], in1=src[:, cut:], op=ALU.mult)
+            width = chunks[k][2]
+            lo = MIRRORED[k]
+            hi = lo + VECTOR_SQUARES[k]
+            return src, dst, lo // RUN, hi // RUN
+
+        def square_scalar(k):
+            squares[k] = square_pool.tile([P, chunks[k][2], PACK], BF16, align_bytes=64, name="squares")
+            src, dst, lo, hi = square_views(k)
+            nc.scalar.activation(out=dst[:, hi:], in_=src[:, hi:], func=ACT.Square)
+
+        def square_mirrored(k):
+            src, dst, lo, hi = square_views(k)
+            step = BLOCK // RUN
+            for i in blocks(k):
+                cols = slice(step * i, step * (i + 1))
+                nc.vector.tensor_tensor(
+                    out=dst[:, cols],
+                    in0=x_mirror[k, i][:].rearrange("p t (c i) -> p c t i", i=RUN),
+                    in1=src[:, cols],
+                    op=ALU.mult,
+                )
+
+        def square_vector(k):
+            src, dst, lo, hi = square_views(k)
+            if hi > lo:
+                nc.vector.tensor_tensor(out=dst[:, lo:hi], in0=src[:, lo:hi], in1=src[:, lo:hi], op=ALU.mult)
+            if hi > lo > 0:
+                n = hi * RUN - 1
+                nc.gpsimd.tensor_copy(out=gate[:], in_=squares[k][:, n, :])
 
         def quantise(k):
             width = chunks[k][2]
@@ -81,40 +125,76 @@ def tile_gdn_kernel(tc, x, beta, gamma_words, gamma_scales, out):
                 in_=squares[k][:].rearrange("p c t -> p (c t)"),
             )
 
-        def multiply_mx(k):
-            for t in range(PACK):
-                for h in range(chunks[k][2] // N_PASS):
-                    mixes[k, t, h] = psum.tile([P, N_PASS], F32, name="mix")
-                    nc.tensor.matmul_mx(
-                        out=mixes[k, t, h][:],
-                        lhsT=g_words[:, 2 * P * t : 2 * P * (t + 1)].bitcast(FP4X4),
-                        lhsT_scale=g_scales[:, P * t : P * (t + 1)],
-                        rhs=codes[k][:, N_PASS * h : N_PASS * (h + 1)].bitcast(FP8X4),
-                        rhs_scale=scales[k][:, N_PASS * h : N_PASS * (h + 1)],
-                        start=True,
-                        stop=True,
+        def passes(k):
+            n_pass = min(N_PASS, chunks[k][2])
+            return [(t, n, n + n_pass) for n in range(0, chunks[k][2], n_pass) for t in range(PACK)]
+
+        def multiply_mx(k, t, lo, hi):
+            mixes[k, t, lo] = psum.tile([P, hi - lo], F32, name="mix")
+            nc.tensor.matmul_mx(
+                out=mixes[k, t, lo][:],
+                lhsT=g_words[:, 2 * P * t : 2 * P * (t + 1)].bitcast(FP4X4),
+                lhsT_scale=g_scales[:, P * t : P * (t + 1)],
+                rhs=codes[k][:, lo:hi].bitcast(FP8X4),
+                rhs_scale=scales[k][:, lo:hi],
+                start=True,
+                stop=True,
+            )
+
+        def reciprocal_root(k, t, lo, hi):
+            nc.scalar.activation(
+                out=rnorms[k][:, t, lo:hi],
+                in_=mixes[k, t, lo][:],
+                func=ACT.Abs_reciprocal_sqrt,
+                bias=beta_f32[:, t : t + 1],
+                scale=1.0,
+            )
+
+        def product_mirrored(k):
+            if MIRRORED[k]:
+                result = stores.tile([P, PACK, N_PASS], F32, name="result")
+                for i in blocks(k):
+                    cols = slice(BLOCK * i, BLOCK * (i + 1))
+                    nc.vector.tensor_tensor(
+                        out=result[:, :, cols], in0=x_mirror[k, i][:], in1=rnorms[k][:, :, cols], op=ALU.mult
                     )
+                store(k, 0, result)
 
-        def reciprocal_root(k, t):
-            rnorms[k, t] = norms.tile([P, chunks[k][2]], F32, name="rnorm")
-            for h in range(chunks[k][2] // N_PASS):
-                nc.scalar.activation(
-                    out=rnorms[k, t][:, N_PASS * h : N_PASS * (h + 1)],
-                    in_=mixes[k, t, h][:],
-                    func=ACT.Abs_reciprocal_sqrt,
-                    bias=beta_f32[:, t : t + 1],
-                    scale=1.0,
+        def product_rest(k):
+            width = chunks[k][2]
+            lo = MIRRORED[k]
+            mid = lo + POOL_PRODUCTS[k]
+            result = stores.tile([P, PACK, width - lo], F32, name="result")
+            if mid > lo:
+                for t in range(0, PACK, 2):
+                    nc.gpsimd.tensor_tensor(
+                        out=result[:, t : t + 2, : mid - lo],
+                        in0=x_word[k][:, t : t + 2, lo:mid],
+                        in1=rnorms[k][:, t : t + 2, lo:mid],
+                        op=ALU.mult,
+                    )
+            if mid < width:
+                nc.vector.tensor_tensor(
+                    out=result[:, :, mid - lo :], in0=x_word[k][:, :, mid:], in1=rnorms[k][:, :, mid:], op=ALU.mult
                 )
+            store(k, lo, result)
 
-        def normalise(k, t):
+        def product_stream(k):
             b, n0, width = chunks[k]
-            result = stores.tile([P, width], F32, name="result")
-            nc.vector.tensor_tensor(out=result[:], in0=x_word[k][:, t, :], in1=rnorms[k, t][:], op=ALU.mult)
-            nc.sync.dma_start(out=out_by_word[b, :, t, n0 : n0 + width], in_=result[:])
+            for t in range(PACK):
+                result = stores.tile([P, width], F32, bufs=8, name="streamed")
+                nc.vector.tensor_tensor(out=result[:], in0=x_word[k][:, t, :], in1=rnorms[k][:, t, :], op=ALU.mult)
+                nc.sync.dma_start(out=out_by_word[b, :, t, n0 : n0 + width], in_=result[:])
+
+        def store(k, n, result):
+            b, n0, width = chunks[k]
+            nc.sync.dma_start(out=out_by_word[b, :, :, n0 + n : n0 + n + result.shape[2]], in_=result[:])
 
         load(0)
         g_words_raw = const.tile([P, 2 * CHANNELS], U8, align_bytes=64)
         g_scales_raw = const.tile([P, CHANNELS], U8, align_bytes=64)
+        one = const.tile([P, 1], F32)
+        nc.vector.memset(one[:], 1.0)
         nc.vector.memset(g_scales_raw[:].bitcast(I32), 0)
         nc.sync.dma_start(out=g_words_raw[:].bitcast(I32), in_=gamma_words[0].bitcast(I32))
         for quadrant in range(4):
@@ -128,13 +208,15 @@ def tile_gdn_kernel(tc, x, beta, gamma_words, gamma_scales, out):
         beta_bf16 = const.tile([P, PACK], BF16)
         nc.scalar.dma_start(out=beta_bf16[:], in_=beta.rearrange("a (p t) h w -> p (a t h w)", t=PACK))
         beta_f32 = const.tile([P, PACK], F32)
-        nc.vector.tensor_copy(out=beta_f32[:], in_=beta_bf16[:])
+        identity = const.tile([P, P], BF16)
+        make_identity(nc, identity[:])
+        gate = const.tile([P, PACK], BF16)
 
-        one = const.tile([P, 1], F32)
-        nc.vector.memset(one[:], 1.0)
         nc.scalar.activation(out=one[:], in_=one[:], func=ACT.Abs_reciprocal_sqrt)
 
-        square(0)
+        square_scalar(0)
+        square_vector(0)
+        nc.vector.tensor_copy(out=beta_f32[:], in_=beta_bf16[:])
 
         g_words = const.tile([P, 2 * CHANNELS], U8, align_bytes=64)
         g_scales = const.tile([P, CHANNELS], U8, align_bytes=64)
@@ -149,19 +231,33 @@ def tile_gdn_kernel(tc, x, beta, gamma_words, gamma_scales, out):
             )
 
         quantise(0)
-        multiply_mx(0)
         for k in range(len(chunks)):
             if k < last:
-                square(k + 1)
-            if k > 0:
-                normalise(k - 1, 2)
-                normalise(k - 1, 3)
-            for t in range(PACK):
-                reciprocal_root(k, t)
+                square_scalar(k + 1)
+                square_vector(k + 1)
+            if first <= k < last and MIRRORED[k + 1]:
+                mirror(k + 1, 0)
+            if k - 1 in mirrored[:-1]:
+                product_mirrored(k - 1)
+            todo = passes(k)
+            for item in todo[:AHEAD]:
+                multiply_mx(k, *item)
             if k < last:
+                if k >= first and MIRRORED[k + 1]:
+                    mirror(k + 1, 1)
+                square_mirrored(k + 1)
                 quantise(k + 1)
-                multiply_mx(k + 1)
-            normalise(k, 0)
-            normalise(k, 1)
-        normalise(last, 2)
-        normalise(last, 3)
+            if 0 < k <= streamed:
+                product_rest(k - 1)
+            rnorms[k] = norms.tile([P, PACK, chunks[k][2]], F32, name="rnorm")
+            for i in range(len(todo)):
+                reciprocal_root(k, *todo[i])
+                if i + AHEAD < len(todo):
+                    multiply_mx(k, *todo[i + AHEAD])
+            if k + 2 == first:
+                mirror(first, 0)
+                mirror(first, 1)
+            if k == mirrored[-1]:
+                product_mirrored(k)
+            if k >= streamed:
+                product_stream(k)

@@ -19,12 +19,12 @@ BATCH = 2
 CHANNELS = 512
 POSITIONS = 64 * 64
 N_PASS = 512
-CHUNK_WIDTHS = ((512, 512, 1024, 1024, 1024), (1024, 1024, 1024, 512, 512))
+CHUNK_WIDTHS = ((512, 512, 1024, 1024, 1024), (1024, 1024, 512, 512, 512, 512))
 RUN = 8
 BLOCK = 256
-MIRRORED = (0, 0, 512, 512, 512, 512, 512, 512, 0, 0)
-VECTOR_SQUARES = (192, 192, 128, 128, 128, 128, 128, 128, 192, 192)
-POOL_PRODUCTS = (256, 256, 448, 448, 448, 448, 320, 256, 0, 0)
+MIRRORED = (0, 0, 512, 512, 512, 512, 512, 256, 0, 0, 0)
+VECTOR_SQUARES = (192, 192, 128, 128, 128, 128, 128, 64, 128, 128, 128)
+POOL_PRODUCTS = (256, 256, 448, 448, 448, 448, 448, 192, 0, 0, 0)
 AHEAD = 3
 
 FLOPS = 2 * CHANNELS * CHANNELS * BATCH * POSITIONS
@@ -152,7 +152,7 @@ def tile_gdn_kernel(tc, x, beta, gamma_words, gamma_scales, out):
 
         def product_mirrored(k):
             if MIRRORED[k]:
-                result = stores.tile([P, PACK, N_PASS], F32, name="result")
+                result = stores.tile([P, PACK, MIRRORED[k]], F32, name="result")
                 for i in blocks(k):
                     cols = slice(BLOCK * i, BLOCK * (i + 1))
                     nc.vector.tensor_tensor(
@@ -243,8 +243,9 @@ def tile_gdn_kernel(tc, x, beta, gamma_words, gamma_scales, out):
             for item in todo[:AHEAD]:
                 multiply_mx(k, *item)
             if k < last:
-                if k >= first and MIRRORED[k + 1]:
-                    mirror(k + 1, 1)
+                if k >= first:
+                    for i in blocks(k + 1)[1:]:
+                        mirror(k + 1, i)
                 square_mirrored(k + 1)
                 quantise(k + 1)
             if 0 < k <= streamed:
@@ -255,8 +256,8 @@ def tile_gdn_kernel(tc, x, beta, gamma_words, gamma_scales, out):
                 if i + AHEAD < len(todo):
                     multiply_mx(k, *todo[i + AHEAD])
             if k + 2 == first:
-                mirror(first, 0)
-                mirror(first, 1)
+                for i in blocks(first):
+                    mirror(first, i)
             if k == mirrored[-1]:
                 product_mirrored(k)
             if k >= streamed:

@@ -23,7 +23,7 @@ CHUNK_WIDTHS = ((512, 512, 1024, 1024, 1024), (1024, 1024, 512, 512, 512, 512))
 RUN = 8
 BLOCK = 256
 MIRRORED = (0, 0, 512, 512, 512, 512, 512, 256, 0, 0, 0)
-VECTOR_SQUARES = (192, 192, 128, 128, 128, 128, 128, 64, 128, 128, 128)
+VECTOR_SQUARES = (192, 192, 192, 128, 128, 128, 128, 64, 128, 128, 128)
 POOL_PRODUCTS = (256, 256, 448, 448, 448, 448, 448, 192, 0, 0, 0)
 AHEAD = 3
 
@@ -247,9 +247,12 @@ def tile_gdn_kernel(tc, x, beta, gamma_words, gamma_scales, out):
                     for i in blocks(k + 1)[1:]:
                         mirror(k + 1, i)
                 square_mirrored(k + 1)
-                quantise(k + 1)
             if 0 < k <= streamed:
                 product_rest(k - 1)
+            if k > streamed:
+                product_stream(k - 1)
+            if k < last:
+                quantise(k + 1)
             rnorms[k] = norms.tile([P, PACK, chunks[k][2]], F32, name="rnorm")
             for i in range(len(todo)):
                 reciprocal_root(k, *todo[i])
@@ -260,5 +263,4 @@ def tile_gdn_kernel(tc, x, beta, gamma_words, gamma_scales, out):
                     mirror(first, i)
             if k == mirrored[-1]:
                 product_mirrored(k)
-            if k >= streamed:
-                product_stream(k)
+        product_stream(last)

@@ -23,8 +23,8 @@ CHUNK_WIDTHS = ((512, 512, 1024, 1024, 1024), (1024, 1024, 512, 512, 512, 512))
 RUN = 8
 BLOCK = 256
 MIRRORED = (0, 0, 512, 512, 512, 512, 512, 256, 0, 0, 0)
-VECTOR_SQUARES = (192, 192, 192, 128, 128, 128, 128, 64, 128, 128, 128)
-POOL_PRODUCTS = (256, 256, 448, 448, 448, 448, 448, 192, 0, 0, 0)
+VECTOR_SQUARES = (192, 192, 192, 64, 64, 64, 64, 32, 128, 128, 128)
+POOL_PRODUCTS = (192, 192, 320, 320, 320, 320, 320, 128, 0, 0, 0)
 AHEAD = 3
 
 FLOPS = 2 * CHANNELS * CHANNELS * BATCH * POSITIONS

@@ -23,8 +23,8 @@ CHUNK_WIDTHS = ((512, 512, 1024, 1024, 1024), (1024, 1024, 512, 512, 512, 512))
 RUN = 8
 BLOCK = 256
 MIRRORED = (0, 0, 512, 512, 512, 512, 512, 256, 0, 0, 0)
-VECTOR_SQUARES = (192, 192, 192, 64, 64, 64, 64, 32, 128, 128, 128)
-POOL_PRODUCTS = (192, 192, 320, 320, 320, 320, 320, 128, 0, 0, 0)
+VECTOR_SQUARES = (192, 192, 192, 64, 64, 64, 64, 32, 112, 112, 112)
+POOL_PRODUCTS = (192, 192, 384, 384, 384, 384, 288, 0, 0, 0, 0)
 AHEAD = 3
 
 FLOPS = 2 * CHANNELS * CHANNELS * BATCH * POSITIONS
@@ -166,13 +166,9 @@ def tile_gdn_kernel(tc, x, beta, gamma_words, gamma_scales, out):
             mid = lo + POOL_PRODUCTS[k]
             result = stores.tile([P, PACK, width - lo], F32, name="result")
             if mid > lo:
-                for t in range(0, PACK, 2):
-                    nc.gpsimd.tensor_tensor(
-                        out=result[:, t : t + 2, : mid - lo],
-                        in0=x_word[k][:, t : t + 2, lo:mid],
-                        in1=rnorms[k][:, t : t + 2, lo:mid],
-                        op=ALU.mult,
-                    )
+                nc.gpsimd.tensor_tensor(
+                    out=result[:, :, : mid - lo], in0=x_word[k][:, :, lo:mid], in1=rnorms[k][:, :, lo:mid], op=ALU.mult
+                )
             if mid < width:
                 nc.vector.tensor_tensor(
                     out=result[:, :, mid - lo :], in0=x_word[k][:, :, mid:], in1=rnorms[k][:, :, mid:], op=ALU.mult

@@ -22,9 +22,10 @@ N_PASS = 512
 CHUNK_WIDTHS = ((512, 512, 1024, 1024, 1024), (1024, 1024, 512, 512, 512, 512))
 RUN = 8
 BLOCK = 256
-MIRRORED = (0, 0, 512, 512, 512, 512, 512, 256, 0, 0, 0)
-VECTOR_SQUARES = (192, 192, 192, 64, 64, 64, 64, 32, 112, 112, 112)
-POOL_PRODUCTS = (192, 192, 384, 384, 384, 384, 288, 0, 0, 0, 0)
+MIRRORED = (0, 0, 512, 512, 512, 512, 512, 0, 0, 0, 0)
+VECTOR_SQUARES = (192, 192, 256, 64, 64, 64, 64, 128, 112, 112, 112)
+POOL_PRODUCTS = (192, 192, 416, 416, 416, 416, 160, 0, 0, 0, 0)
+LOADS = ((512, 512, 1024, 2048), (2048, 2048))
 AHEAD = 3
 
 FLOPS = 2 * CHANNELS * CHANNELS * BATCH * POSITIONS
@@ -63,10 +64,13 @@ def tile_gdn_kernel(tc, x, beta, gamma_words, gamma_scales, out):
         mixes = {}
         rnorms = {}
 
-        def load(k):
-            b, n0, width = chunks[k]
-            x_word[k] = word_pool.tile([P, PACK, width], BF16, name="x_word_%d" % k)
-            nc.sync.dma_start(out=x_word[k][:], in_=x_by_word[b, :, :, n0 : n0 + width])
+        def load(i):
+            b, n0, width = loads[i]
+            tile = word_pool.tile([P, PACK, width], BF16, name="x_word_%d" % i)
+            nc.sync.dma_start(out=tile[:], in_=x_by_word[b, :, :, n0 : n0 + width])
+            for k in range(len(chunks)):
+                if chunks[k][0] == b and n0 <= chunks[k][1] < n0 + width:
+                    x_word[k] = tile[:, :, chunks[k][1] - n0 : chunks[k][1] - n0 + chunks[k][2]]
 
         def blocks(k):
             return range(MIRRORED[k] // BLOCK)
@@ -83,7 +87,7 @@ def tile_gdn_kernel(tc, x, beta, gamma_words, gamma_scales, out):
                 )
 
         def square_views(k):
-            src = x_word[k][:].rearrange("p t (c i) -> p c t i", i=RUN)
+            src = x_word[k].rearrange("p t (c i) -> p c t i", i=RUN)
             dst = squares[k][:].rearrange("p (c i) t -> p c t i", i=RUN)
             width = chunks[k][2]
             lo = MIRRORED[k]
@@ -186,6 +190,10 @@ def tile_gdn_kernel(tc, x, beta, gamma_words, gamma_scales, out):
             b, n0, width = chunks[k]
             nc.sync.dma_start(out=out_by_word[b, :, :, n0 + n : n0 + n + result.shape[2]], in_=result[:])
 
+        loads = []
+        for b in range(BATCH):
+            for i, width in enumerate(LOADS[b]):
+                loads.append((b, sum(LOADS[b][:i]), width))
         load(0)
         g_words_raw = const.tile([P, 2 * CHANNELS], U8, align_bytes=64)
         g_scales_raw = const.tile([P, CHANNELS], U8, align_bytes=64)
@@ -198,8 +206,8 @@ def tile_gdn_kernel(tc, x, beta, gamma_words, gamma_scales, out):
                 out=g_scales_raw[32 * quadrant : 32 * quadrant + 4, :].bitcast(I32),
                 in_=gamma_scales[0, 4 * quadrant : 4 * quadrant + 4, :].bitcast(I32),
             )
-        for k in range(1, len(chunks)):
-            load(k)
+        for i in range(1, len(loads)):
+            load(i)
 
         beta_bf16 = const.tile([P, PACK], BF16)
         nc.scalar.dma_start(out=beta_bf16[:], in_=beta.rearrange("a (p t) h w -> p (a t h w)", t=PACK))
@@ -231,15 +239,16 @@ def tile_gdn_kernel(tc, x, beta, gamma_words, gamma_scales, out):
             if k < last:
                 square_scalar(k + 1)
                 square_vector(k + 1)
-            if first <= k < last and MIRRORED[k + 1]:
-                mirror(k + 1, 0)
+            if first <= k < last:
+                for i in blocks(k + 1)[: 2 if k == first else 1]:
+                    mirror(k + 1, i)
             if k - 1 in mirrored[:-1]:
                 product_mirrored(k - 1)
             todo = passes(k)
             for item in todo[:AHEAD]:
                 multiply_mx(k, *item)
             if k < last:
-                if k >= first:
+                if k > first:
                     for i in blocks(k + 1)[1:]:
                         mirror(k + 1, i)
                 square_mirrored(k + 1)

@@ -23,7 +23,7 @@ CHUNK_WIDTHS = ((512, 512, 1024, 1024, 1024), (1024, 1024, 512, 512, 512, 512))
 RUN = 8
 BLOCK = 256
 MIRRORED = (0, 0, 512, 512, 512, 512, 512, 0, 0, 0, 0)
-VECTOR_SQUARES = (192, 192, 256, 64, 64, 64, 64, 128, 112, 112, 112)
+VECTOR_SQUARES = (192, 192, 256, 96, 96, 96, 96, 128, 128, 128, 128)
 POOL_PRODUCTS = (192, 192, 416, 416, 416, 416, 160, 0, 0, 0, 0)
 LOADS = ((512, 512, 1024, 2048), (2048, 2048))
 AHEAD = 3

@@ -22,10 +22,12 @@ N_PASS = 512
 CHUNK_WIDTHS = ((512, 512, 1024, 1024, 1024), (1024, 1024, 512, 512, 512, 512))
 RUN = 8
 BLOCK = 256
-MIRRORED = (0, 0, 512, 512, 512, 512, 512, 0, 0, 0, 0)
-VECTOR_SQUARES = (192, 192, 256, 96, 96, 96, 96, 128, 128, 128, 128)
-POOL_PRODUCTS = (192, 192, 416, 416, 416, 416, 160, 0, 0, 0, 0)
+MIRRORED = (0, 0, 512, 512, 512, 512, 512, 256, 0, 0, 0)
+VECTOR_SQUARES = (192, 192, 256, 96, 96, 96, 64, 0, 64, 128, 128)
+POOL_PRODUCTS = (192, 192, 416, 416, 416, 352, 96, 96, 0, 0, 0)
 LOADS = ((512, 512, 1024, 2048), (2048, 2048))
+WHOLE = (7,)
+STORES = 6
 AHEAD = 3
 
 FLOPS = 2 * CHANNELS * CHANNELS * BATCH * POSITIONS
@@ -51,7 +53,7 @@ def tile_gdn_kernel(tc, x, beta, gamma_words, gamma_scales, out):
         square_pool = ctx.enter_context(tc.tile_pool(name="square_pool", bufs=3))
         code_pool = ctx.enter_context(tc.tile_pool(name="code_pool", bufs=3))
         norms = ctx.enter_context(tc.tile_pool(name="norms", bufs=3))
-        stores = ctx.enter_context(tc.tile_pool(name="stores", bufs=6))
+        stores = ctx.enter_context(tc.tile_pool(name="stores", bufs=STORES))
         psum = ctx.enter_context(tc.psum_pool(name="psum", bufs=AHEAD))
         mirrors = ctx.enter_context(tc.psum_pool(name="mirrors", bufs=5))
         ctx.enter_context(tc.manual_schedule())
@@ -63,6 +65,7 @@ def tile_gdn_kernel(tc, x, beta, gamma_words, gamma_scales, out):
         scales = {}
         mixes = {}
         rnorms = {}
+        results = {}
 
         def load(i):
             b, n0, width = loads[i]
@@ -155,29 +158,34 @@ def tile_gdn_kernel(tc, x, beta, gamma_words, gamma_scales, out):
             )
 
         def product_mirrored(k):
-            if MIRRORED[k]:
-                result = stores.tile([P, PACK, MIRRORED[k]], F32, name="result")
-                for i in blocks(k):
-                    cols = slice(BLOCK * i, BLOCK * (i + 1))
-                    nc.vector.tensor_tensor(
-                        out=result[:, :, cols], in0=x_mirror[k, i][:], in1=rnorms[k][:, :, cols], op=ALU.mult
-                    )
-                store(k, 0, result)
+            lo = MIRRORED[k]
+            whole = lo and k in WHOLE
+            if whole:
+                results[k] = stores.tile([P, PACK, chunks[k][2]], F32, bufs=2, name="whole")
+            elif lo:
+                results[k] = stores.tile([P, PACK, lo], F32, name="result")
+            for i in blocks(k):
+                cols = slice(BLOCK * i, BLOCK * (i + 1))
+                nc.vector.tensor_tensor(
+                    out=results[k][:, :, cols], in0=x_mirror[k, i][:], in1=rnorms[k][:, :, cols], op=ALU.mult
+                )
+            if lo and not whole:
+                store(k, 0, results[k])
+
+        def product(engine, result, k, lo, hi):
+            if lo < hi:
+                engine.tensor_tensor(out=result, in0=x_word[k][:, :, lo:hi], in1=rnorms[k][:, :, lo:hi], op=ALU.mult)
 
         def product_rest(k):
             width = chunks[k][2]
             lo = MIRRORED[k]
             mid = lo + POOL_PRODUCTS[k]
-            result = stores.tile([P, PACK, width - lo], F32, name="result")
-            if mid > lo:
-                nc.gpsimd.tensor_tensor(
-                    out=result[:, :, : mid - lo], in0=x_word[k][:, :, lo:mid], in1=rnorms[k][:, :, lo:mid], op=ALU.mult
-                )
-            if mid < width:
-                nc.vector.tensor_tensor(
-                    out=result[:, :, mid - lo :], in0=x_word[k][:, :, mid:], in1=rnorms[k][:, :, mid:], op=ALU.mult
-                )
-            store(k, lo, result)
+            base = 0 if k in WHOLE else lo
+            if k not in WHOLE:
+                results[k] = stores.tile([P, PACK, width - lo], F32, name="result")
+            product(nc.gpsimd, results[k][:, :, lo - base : mid - base], k, lo, mid)
+            product(nc.vector, results[k][:, :, mid - base :], k, mid, width)
+            store(k, base, results[k])
 
         def product_stream(k):
             b, n0, width = chunks[k]

from contextlib import ExitStack

import concourse.mybir as mybir
from concourse.masks import make_identity

F32 = mybir.dt.float32
BF16 = mybir.dt.bfloat16
I32 = mybir.dt.int32
U32 = mybir.dt.uint32
U8 = mybir.dt.uint8
FP8X4 = mybir.dt.float8_e4m3fn_x4
FP4X4 = mybir.dt.float4_e2m1fn_x4
ACT = mybir.ActivationFunctionType
ALU = mybir.AluOpType

P = 128
PACK = 4
BATCH = 2
CHANNELS = 512
POSITIONS = 64 * 64
N_PASS = 512
CHUNK_WIDTHS = ((512, 512, 1024, 1024, 1024), (1024, 1024, 512, 512, 512, 512))
RUN = 8
BLOCK = 256
MIRRORED = (0, 0, 512, 512, 512, 512, 512, 256, 0, 0, 0)
VECTOR_SQUARES = (192, 192, 256, 96, 96, 96, 64, 0, 64, 128, 128)
POOL_PRODUCTS = (192, 192, 416, 416, 416, 352, 96, 96, 0, 0, 0)
LOADS = ((512, 512, 1024, 2048), (2048, 2048))
WHOLE = (7,)
STORES = 6
AHEAD = 3

FLOPS = 2 * CHANNELS * CHANNELS * BATCH * POSITIONS


def tile_gdn_kernel(tc, x, beta, gamma_words, gamma_scales, out):
    nc = tc.nc
    x_by_word = x.rearrange("b (p t) h w -> b p t (h w)", t=PACK)
    out_by_word = out.rearrange("b (p t) h w -> b p t (h w)", t=PACK)
    chunks = []
    for b in range(BATCH):
        assert sum(CHUNK_WIDTHS[b]) == POSITIONS
        for i, width in enumerate(CHUNK_WIDTHS[b]):
            chunks.append((b, sum(CHUNK_WIDTHS[b][:i]), width))
    last = len(chunks) - 1
    mirrored = [k for k in range(len(chunks)) if MIRRORED[k]]
    first = mirrored[0]
    streamed = mirrored[-1] + 1

    with ExitStack() as ctx:
        const = ctx.enter_context(tc.tile_pool(name="const", bufs=1))
        word_pool = ctx.enter_context(tc.tile_pool(name="word_pool", bufs=1))
        square_pool = ctx.enter_context(tc.tile_pool(name="square_pool", bufs=3))
        code_pool = ctx.enter_context(tc.tile_pool(name="code_pool", bufs=3))
        norms = ctx.enter_context(tc.tile_pool(name="norms", bufs=3))
        stores = ctx.enter_context(tc.tile_pool(name="stores", bufs=STORES))
        psum = ctx.enter_context(tc.psum_pool(name="psum", bufs=AHEAD))
        mirrors = ctx.enter_context(tc.psum_pool(name="mirrors", bufs=5))
        ctx.enter_context(tc.manual_schedule())

        x_word = {}
        x_mirror = {}
        squares = {}
        codes = {}
        scales = {}
        mixes = {}
        rnorms = {}
        results = {}

        def load(i):
            b, n0, width = loads[i]
            tile = word_pool.tile([P, PACK, width], BF16, name="x_word_%d" % i)
            nc.sync.dma_start(out=tile[:], in_=x_by_word[b, :, :, n0 : n0 + width])
            for k in range(len(chunks)):
                if chunks[k][0] == b and n0 <= chunks[k][1] < n0 + width:
                    x_word[k] = tile[:, :, chunks[k][1] - n0 : chunks[k][1] - n0 + chunks[k][2]]

        def blocks(k):
            return range(MIRRORED[k] // BLOCK)

        def mirror(k, i):
            x_mirror[k, i] = mirrors.tile([P, PACK, BLOCK], BF16, name="x_mirror")
            for t in range(0, PACK, 2):
                nc.tensor.matmul(
                    out=x_mirror[k, i][:, t : t + 2, :],
                    lhsT=identity[:],
                    rhs=x_word[k][:, t : t + 2, BLOCK * i : BLOCK * (i + 1)],
                    start=True,
                    stop=True,
                )

        def square_views(k):
            src = x_word[k].rearrange("p t (c i) -> p c t i", i=RUN)
            dst = squares[k][:].rearrange("p (c i) t -> p c t i", i=RUN)
            width = chunks[k][2]
            lo = MIRRORED[k]
            hi = lo + VECTOR_SQUARES[k]
            return src, dst, lo // RUN, hi // RUN

        def square_scalar(k):
            squares[k] = square_pool.tile([P, chunks[k][2], PACK], BF16, align_bytes=64, name="squares")
            src, dst, lo, hi = square_views(k)
            nc.scalar.activation(out=dst[:, hi:], in_=src[:, hi:], func=ACT.Square)

        def square_mirrored(k):
            src, dst, lo, hi = square_views(k)
            step = BLOCK // RUN
            for i in blocks(k):
                cols = slice(step * i, step * (i + 1))
                nc.vector.tensor_tensor(
                    out=dst[:, cols],
                    in0=x_mirror[k, i][:].rearrange("p t (c i) -> p c t i", i=RUN),
                    in1=src[:, cols],
                    op=ALU.mult,
                )

        def square_vector(k):
            src, dst, lo, hi = square_views(k)
            if hi > lo:
                nc.vector.tensor_tensor(out=dst[:, lo:hi], in0=src[:, lo:hi], in1=src[:, lo:hi], op=ALU.mult)
            if hi > lo > 0:
                n = hi * RUN - 1
                nc.gpsimd.tensor_copy(out=gate[:], in_=squares[k][:, n, :])

        def quantise(k):
            width = chunks[k][2]
            codes[k] = code_pool.tile([P, width], U32, align_bytes=64, name="codes")
            scales[k] = code_pool.tile([P, width], U8, align_bytes=64, name="scales")
            nc.vector.quantize_mx(
                out=codes[k][:].bitcast(FP8X4),
                scales=scales[k][:],
                in_=squares[k][:].rearrange("p c t -> p (c t)"),
            )

        def passes(k):
            n_pass = min(N_PASS, chunks[k][2])
            return [(t, n, n + n_pass) for n in range(0, chunks[k][2], n_pass) for t in range(PACK)]

        def multiply_mx(k, t, lo, hi):
            mixes[k, t, lo] = psum.tile([P, hi - lo], F32, name="mix")
            nc.tensor.matmul_mx(
                out=mixes[k, t, lo][:],
                lhsT=g_words[:, 2 * P * t : 2 * P * (t + 1)].bitcast(FP4X4),
                lhsT_scale=g_scales[:, P * t : P * (t + 1)],
                rhs=codes[k][:, lo:hi].bitcast(FP8X4),
                rhs_scale=scales[k][:, lo:hi],
                start=True,
                stop=True,
            )

        def reciprocal_root(k, t, lo, hi):
            nc.scalar.activation(
                out=rnorms[k][:, t, lo:hi],
                in_=mixes[k, t, lo][:],
                func=ACT.Abs_reciprocal_sqrt,
                bias=beta_f32[:, t : t + 1],
                scale=1.0,
            )

        def product_mirrored(k):
            lo = MIRRORED[k]
            whole = lo and k in WHOLE
            if whole:
                results[k] = stores.tile([P, PACK, chunks[k][2]], F32, bufs=2, name="whole")
            elif lo:
                results[k] = stores.tile([P, PACK, lo], F32, name="result")
            for i in blocks(k):
                cols = slice(BLOCK * i, BLOCK * (i + 1))
                nc.vector.tensor_tensor(
                    out=results[k][:, :, cols], in0=x_mirror[k, i][:], in1=rnorms[k][:, :, cols], op=ALU.mult
                )
            if lo and not whole:
                store(k, 0, results[k])

        def product(engine, result, k, lo, hi):
            if lo < hi:
                engine.tensor_tensor(out=result, in0=x_word[k][:, :, lo:hi], in1=rnorms[k][:, :, lo:hi], op=ALU.mult)

        def product_rest(k):
            width = chunks[k][2]
            lo = MIRRORED[k]
            mid = lo + POOL_PRODUCTS[k]
            base = 0 if k in WHOLE else lo
            if k not in WHOLE:
                results[k] = stores.tile([P, PACK, width - lo], F32, name="result")
            product(nc.gpsimd, results[k][:, :, lo - base : mid - base], k, lo, mid)
            product(nc.vector, results[k][:, :, mid - base :], k, mid, width)
            store(k, base, results[k])

        def product_stream(k):
            b, n0, width = chunks[k]
            for t in range(PACK):
                result = stores.tile([P, width], F32, bufs=8, name="streamed")
                nc.vector.tensor_tensor(out=result[:], in0=x_word[k][:, t, :], in1=rnorms[k][:, t, :], op=ALU.mult)
                nc.sync.dma_start(out=out_by_word[b, :, t, n0 : n0 + width], in_=result[:])

        def store(k, n, result):
            b, n0, width = chunks[k]
            nc.sync.dma_start(out=out_by_word[b, :, :, n0 + n : n0 + n + result.shape[2]], in_=result[:])

        loads = []
        for b in range(BATCH):
            for i, width in enumerate(LOADS[b]):
                loads.append((b, sum(LOADS[b][:i]), width))
        load(0)
        g_words_raw = const.tile([P, 2 * CHANNELS], U8, align_bytes=64)
        g_scales_raw = const.tile([P, CHANNELS], U8, align_bytes=64)
        one = const.tile([P, 1], F32)
        nc.vector.memset(one[:], 1.0)
        nc.vector.memset(g_scales_raw[:].bitcast(I32), 0)
        nc.sync.dma_start(out=g_words_raw[:].bitcast(I32), in_=gamma_words[0].bitcast(I32))
        for quadrant in range(4):
            nc.sync.dma_start(
                out=g_scales_raw[32 * quadrant : 32 * quadrant + 4, :].bitcast(I32),
                in_=gamma_scales[0, 4 * quadrant : 4 * quadrant + 4, :].bitcast(I32),
            )
        for i in range(1, len(loads)):
            load(i)

        beta_bf16 = const.tile([P, PACK], BF16)
        nc.scalar.dma_start(out=beta_bf16[:], in_=beta.rearrange("a (p t) h w -> p (a t h w)", t=PACK))
        beta_f32 = const.tile([P, PACK], F32)
        identity = const.tile([P, P], BF16)
        make_identity(nc, identity[:])
        gate = const.tile([P, PACK], BF16)

        nc.scalar.activation(out=one[:], in_=one[:], func=ACT.Abs_reciprocal_sqrt)

        square_scalar(0)
        square_vector(0)
        nc.vector.tensor_copy(out=beta_f32[:], in_=beta_bf16[:])

        g_words = const.tile([P, 2 * CHANNELS], U8, align_bytes=64)
        g_scales = const.tile([P, CHANNELS], U8, align_bytes=64)
        for t in range(PACK):
            nc.vector.tensor_copy(
                out=g_words[:, 2 * P * t : 2 * P * (t + 1)].rearrange("p (m e) -> p m e", e=2),
                in_=g_words_raw[:].rearrange("p (m t e) -> p t m e", t=PACK, e=2)[:, t],
            )
            nc.vector.tensor_copy(
                out=g_scales[:, P * t : P * (t + 1)],
                in_=g_scales_raw[:].rearrange("p (m t) -> p t m", t=PACK)[:, t],
            )

        quantise(0)
        for k in range(len(chunks)):
            if k < last:
                square_scalar(k + 1)
                square_vector(k + 1)
            if first <= k < last:
                for i in blocks(k + 1)[: 2 if k == first else 1]:
                    mirror(k + 1, i)
            if k - 1 in mirrored[:-1]:
                product_mirrored(k - 1)
            todo = passes(k)
            for item in todo[:AHEAD]:
                multiply_mx(k, *item)
            if k < last:
                if k > first:
                    for i in blocks(k + 1)[1:]:
                        mirror(k + 1, i)
                square_mirrored(k + 1)
            if 0 < k <= streamed:
                product_rest(k - 1)
            if k > streamed:
                product_stream(k - 1)
            if k < last:
                quantise(k + 1)
            rnorms[k] = norms.tile([P, PACK, chunks[k][2]], F32, name="rnorm")
            for i in range(len(todo)):
                reciprocal_root(k, *todo[i])
                if i + AHEAD < len(todo):
                    multiply_mx(k, *todo[i + AHEAD])
            if k + 2 == first:
                for i in blocks(first):
                    mirror(first, i)
            if k == mirrored[-1]:
                product_mirrored(k)
        product_stream(last)
